import numpy as np
import ml_dtypes

BF16 = ml_dtypes.bfloat16


def bf(x):
    return np.asarray(x, np.float32).astype(BF16)


def f32(x):
    return np.asarray(x, np.float32)


def f64(x):
    return np.asarray(x).astype(np.float64)


def striped(idx):
    return np.tile(idx.reshape(-1, 16).T, (8, 1))


C, S, N = 512, 2048, 512
EPS = 1e-5


def setup_inputs():
    noise = np.random.standard_normal((C, S))
    spread = 0.5 + np.random.random_sample((1, S))
    lift = 0.5 * np.random.standard_normal((1, S))
    shift = 0.5 * np.random.standard_normal((C, 1))
    return {"wte": f32(spread * noise + lift + shift), "offs": striped(np.random.permutation(np.tile(np.arange(S), 2))[:N])}


def reference(wte, offs):
    idx = offs[:16].T.reshape(-1)
    t = f64(wte)
    m = t.mean(axis=0, keepdims=True)
    r = 1.0 / np.sqrt(((t - m) ** 2).mean(axis=0, keepdims=True) + EPS)
    e = (t - m) * r
    avg = t.mean(axis=1, keepdims=True)
    return e[:, idx] + (-avg)

@@ -1,0 +1,113 @@
+import concourse.mybir as mybir
+from concourse.masks import make_identity
+
+F32 = mybir.dt.float32
+U16 = mybir.dt.uint16
+FUNC = mybir.ActivationFunctionType
+ALU = mybir.AluOpType
+
+P = 128
+C, S, N = 512, 2048, 512
+EPS = 1e-5
+BANK = 512
+CHANNEL_BLOCKS = C // P
+GROUPS = S // BANK
+PAIRS_IN_GROUP = 2
+BLOCKS_IN_PAIR = 2
+
+
+def tile_gdw_kernel(tc, wte, offs, out):
+    nc = tc.nc
+    with (
+        tc.tile_pool(name="held", bufs=1) as held,
+        tc.tile_pool(name="rows", bufs=4) as rows,
+        tc.tile_pool(name="norm", bufs=8) as norm,
+        tc.tile_pool(name="small", bufs=8) as small,
+        tc.psum_pool(name="flipped", bufs=6) as flipped,
+        tc.psum_pool(name="back", bufs=2) as back,
+    ):
+        offsets = held.tile([P, N // 16], U16, name="offsets")
+        nc.sync.dma_start(offsets[:], offs)
+
+        raw = [held.tile([P, S], F32, name=f"raw{b}") for b in range(CHANNEL_BLOCKS)]
+        for g in range(GROUPS):
+            for b in range(CHANNEL_BLOCKS):
+                nc.sync.dma_start(
+                    raw[b][:, g * BANK : (g + 1) * BANK],
+                    wte[b * P : (b + 1) * P, g * BANK : (g + 1) * BANK],
+                )
+
+        identity = held.tile([P, P], F32, name="identity")
+        make_identity(nc, identity[:])
+        eps = held.tile([P, 1], F32, name="eps")
+        nc.vector.memset(eps[:], EPS)
+        zeros = held.tile([P, N], F32, name="zeros")
+        nc.gpsimd.memset(zeros[:], 0.0)
+
+        minus_avg_row = []
+        for b in range(CHANNEL_BLOCKS):
+            folded = rows.tile([P, BANK], F32, name="folded")
+            nc.gpsimd.tensor_add(folded[:], raw[b][:, 0:BANK], raw[b][:, BANK : 2 * BANK])
+            for g in range(2, GROUPS):
+                nc.gpsimd.tensor_add(folded[:], folded[:], raw[b][:, g * BANK : (g + 1) * BANK])
+            scaled = rows.tile([P, BANK], F32, name="scaled")
+            minus_avg = small.tile([P, 1], F32, name="minus_avg")
+            nc.scalar.activation(scaled[:], folded[:], FUNC.Copy, scale=-1.0 / S, accum_out=minus_avg[:])
+            spread = rows.tile([P, N], F32, name="spread")
+            nc.gpsimd.tensor_scalar_add(spread[:], zeros[:], minus_avg[:])
+            minus_avg_row.append(spread)
+
+        e = [held.tile([P, S], F32, name=f"e{b}") for b in range(CHANNEL_BLOCKS)]
+
+        for g in range(GROUPS):
+            normed = []
+            for pair in range(PAIRS_IN_GROUP):
+                words = []
+                mean_var = small.tile([P, BLOCKS_IN_PAIR, 2], F32, name="mean_var")
+                for k in range(BLOCKS_IN_PAIR):
+                    first_word = g * BANK + (pair * BLOCKS_IN_PAIR + k) * P
+                    flipped_block = flipped.tile([P, C], F32, name="flipped_block")
+                    for b in range(CHANNEL_BLOCKS):
+                        nc.tensor.transpose(
+                            flipped_block[:, b * P : (b + 1) * P],
+                            raw[b][:, first_word : first_word + P],
+                            identity[:],
+                        )
+                    stats = small.tile([P, 6], F32, name="stats")
+                    nc.vector.bn_stats(stats[:], flipped_block[:])
+                    nc.vector.bn_aggr(mean_var[:, k, :], stats[:])
+                    words.append(flipped_block)
+
+                std = small.tile([P, BLOCKS_IN_PAIR], F32, name="std")
+                nc.scalar.activation(std[:], mean_var[:, :, 1], FUNC.Sqrt, bias=eps[:])
+                rstd = small.tile([P, BLOCKS_IN_PAIR], F32, name="rstd")
+                nc.vector.reciprocal(rstd[:], std[:])
+
+                for k in range(BLOCKS_IN_PAIR):
+                    shift = small.tile([P, 1], F32, name="shift")
+                    nc.vector.tensor_scalar(
+                        shift[:], mean_var[:, k, 0:1], rstd[:, k : k + 1], -1.0, ALU.mult, ALU.mult
+                    )
+                    normed_block = norm.tile([P, C], F32, name="normed_block")
+                    nc.scalar.activation(
+                        normed_block[:], words[k][:], FUNC.Identity, bias=shift[:], scale=rstd[:, k : k + 1]
+                    )
+                    normed.append(normed_block)
+
+            for b in range(CHANNEL_BLOCKS):
+                e_bank = back.tile([P, BANK], F32, name="e_bank")
+                for i, normed_block in enumerate(normed):
+                    nc.tensor.transpose(
+                        e_bank[:, i * P : (i + 1) * P],
+                        normed_block[:, b * P : (b + 1) * P],
+                        identity[:],
+                    )
+                if b % 2 == 0:
+                    nc.scalar.copy(e[b][:, g * BANK : (g + 1) * BANK], e_bank[:])
+                else:
+                    nc.vector.tensor_copy(e[b][:, g * BANK : (g + 1) * BANK], e_bank[:])
+
+        for b in range(CHANNEL_BLOCKS):
+            picked = rows.tile([P, N], F32, name="picked")
+            nc.vector.tensor_tensor(picked[:], e[b][:].indirect(offsets[:]), minus_avg_row[b][:], ALU.add)
+            nc.sync.dma_start(out[b * P : (b + 1) * P, :], picked[:])

@@ -5,15 +5,17 @@ F32 = mybir.dt.float32
 U16 = mybir.dt.uint16
 FUNC = mybir.ActivationFunctionType
 ALU = mybir.AluOpType
+AXIS = mybir.AxisListType
 
 P = 128
 C, S, N = 512, 2048, 512
 EPS = 1e-5
 BANK = 512
+PSUM_BANKS = 8
 CHANNEL_BLOCKS = C // P
 GROUPS = S // BANK
-PAIRS_IN_GROUP = 2
-BLOCKS_IN_PAIR = 2
+BLOCKS_IN_GROUP = BANK // P
+PAIRS = S // (2 * P)
 
 
 def tile_gdw_kernel(tc, wte, offs, out):
@@ -21,10 +23,8 @@ def tile_gdw_kernel(tc, wte, offs, out):
     with (
         tc.tile_pool(name="held", bufs=1) as held,
         tc.tile_pool(name="rows", bufs=4) as rows,
-        tc.tile_pool(name="norm", bufs=8) as norm,
-        tc.tile_pool(name="small", bufs=8) as small,
-        tc.psum_pool(name="flipped", bufs=6) as flipped,
-        tc.psum_pool(name="back", bufs=2) as back,
+        tc.tile_pool(name="small", bufs=6) as small,
+        tc.psum_pool(name="psum", bufs=PSUM_BANKS) as psum,
     ):
         offsets = held.tile([P, N // 16], U16, name="offsets")
         nc.sync.dma_start(offsets[:], offs)
@@ -41,73 +41,110 @@ def tile_gdw_kernel(tc, wte, offs, out):
         make_identity(nc, identity[:])
         eps = held.tile([P, 1], F32, name="eps")
         nc.vector.memset(eps[:], EPS)
-        zeros = held.tile([P, N], F32, name="zeros")
-        nc.gpsimd.memset(zeros[:], 0.0)
 
+        normed = [held.tile([P, C], F32, name=f"normed{j}") for j in range(2 * PAIRS)]
+        minus_avg_parts = held.tile([P, CHANNEL_BLOCKS, GROUPS], F32, name="minus_avg_parts")
+        flipped, mean_var, std, rstd, shift = {}, {}, {}, {}, {}
+
+        def flip_pair(p):
+            flipped[p] = []
+            for k in range(2):
+                first_word = (2 * p + k) * P
+                block = psum.tile([P, C], F32, name="bank")
+                for b in range(CHANNEL_BLOCKS):
+                    nc.tensor.transpose(
+                        block[:, b * P : (b + 1) * P], raw[b][:, first_word : first_word + P], identity[:]
+                    )
+                flipped[p].append(block)
+
+        def measure_pair(p):
+            mean_var[p] = small.tile([P, 2, 2], F32, name="mean_var")
+            for k in range(2):
+                stats = small.tile([P, 6], F32, name="stats")
+                nc.vector.bn_stats(stats[:], flipped[p][k][:])
+                nc.vector.bn_aggr(mean_var[p][:, k, :], stats[:])
+
+        def root_pair(p):
+            std[p] = small.tile([P, 2], F32, name="std")
+            nc.scalar.activation(std[p][:], mean_var[p][:, :, 1], FUNC.Sqrt, bias=eps[:])
+
+        def invert_pair(p):
+            rstd[p] = small.tile([P, 2], F32, name="rstd")
+            nc.vector.reciprocal(rstd[p][:], std[p][:])
+            shift[p] = small.tile([P, 1], F32, name="shift")
+            nc.vector.tensor_scalar(
+                shift[p][:], mean_var[p][:, 0, 0:1], rstd[p][:, 0:1], -1.0, ALU.mult, ALU.mult
+            )
+
+        def normalise_pair(p):
+            nc.scalar.activation(
+                normed[2 * p][:], flipped[p][0][:], FUNC.Identity, bias=shift[p][:], scale=rstd[p][:, 0:1]
+            )
+            nc.vector.tensor_scalar(
+                normed[2 * p + 1][:],
+                flipped[p][1][:],
+                mean_var[p][:, 1, 0:1],
+                rstd[p][:, 1:2],
+                ALU.subtract,
+                ALU.mult,
+            )
+
+        def sum_rows(p):
+            g = p // 2
+            for b in (2 * (p % 2), 2 * (p % 2) + 1):
+                scaled = rows.tile([P, BANK], F32, name="scaled")
+                nc.scalar.activation(
+                    scaled[:],
+                    raw[b][:, g * BANK : (g + 1) * BANK],
+                    FUNC.Copy,
+                    scale=-1.0 / S,
+                    accum_out=minus_avg_parts[:, b, g : g + 1],
+                )
+
+        flip_pair(0)
+        flip_pair(1)
+        flip_pair(2)
+        sum_rows(0)
+        sum_rows(1)
+        measure_pair(0)
+        root_pair(0)
+        measure_pair(1)
+        root_pair(1)
+        invert_pair(0)
+        for p in range(PAIRS):
+            if p + 3 < PAIRS:
+                flip_pair(p + 3)
+            normalise_pair(p)
+            if p + 2 < PAIRS:
+                sum_rows(p + 2)
+                measure_pair(p + 2)
+                root_pair(p + 2)
+            if p + 1 < PAIRS:
+                invert_pair(p + 1)
+
+        minus_avg = held.tile([P, CHANNEL_BLOCKS], F32, name="minus_avg")
+        nc.vector.reduce_sum(minus_avg[:], minus_avg_parts[:], axis=AXIS.X)
         minus_avg_row = []
         for b in range(CHANNEL_BLOCKS):
-            folded = rows.tile([P, BANK], F32, name="folded")
-            nc.gpsimd.tensor_add(folded[:], raw[b][:, 0:BANK], raw[b][:, BANK : 2 * BANK])
-            for g in range(2, GROUPS):
-                nc.gpsimd.tensor_add(folded[:], folded[:], raw[b][:, g * BANK : (g + 1) * BANK])
-            scaled = rows.tile([P, BANK], F32, name="scaled")
-            minus_avg = small.tile([P, 1], F32, name="minus_avg")
-            nc.scalar.activation(scaled[:], folded[:], FUNC.Copy, scale=-1.0 / S, accum_out=minus_avg[:])
             spread = rows.tile([P, N], F32, name="spread")
-            nc.gpsimd.tensor_scalar_add(spread[:], zeros[:], minus_avg[:])
+            nc.vector.tensor_copy(spread[:], minus_avg[:, b : b + 1].to_broadcast([P, N]))
             minus_avg_row.append(spread)
 
-        e = [held.tile([P, S], F32, name=f"e{b}") for b in range(CHANNEL_BLOCKS)]
-
-        for g in range(GROUPS):
-            normed = []
-            for pair in range(PAIRS_IN_GROUP):
-                words = []
-                mean_var = small.tile([P, BLOCKS_IN_PAIR, 2], F32, name="mean_var")
-                for k in range(BLOCKS_IN_PAIR):
-                    first_word = g * BANK + (pair * BLOCKS_IN_PAIR + k) * P
-                    flipped_block = flipped.tile([P, C], F32, name="flipped_block")
-                    for b in range(CHANNEL_BLOCKS):
-                        nc.tensor.transpose(
-                            flipped_block[:, b * P : (b + 1) * P],
-                            raw[b][:, first_word : first_word + P],
-                            identity[:],
-                        )
-                    stats = small.tile([P, 6], F32, name="stats")
-                    nc.vector.bn_stats(stats[:], flipped_block[:])
-                    nc.vector.bn_aggr(mean_var[:, k, :], stats[:])
-                    words.append(flipped_block)
-
-                std = small.tile([P, BLOCKS_IN_PAIR], F32, name="std")
-                nc.scalar.activation(std[:], mean_var[:, :, 1], FUNC.Sqrt, bias=eps[:])
-                rstd = small.tile([P, BLOCKS_IN_PAIR], F32, name="rstd")
-                nc.vector.reciprocal(rstd[:], std[:])
-
-                for k in range(BLOCKS_IN_PAIR):
-                    shift = small.tile([P, 1], F32, name="shift")
-                    nc.vector.tensor_scalar(
-                        shift[:], mean_var[:, k, 0:1], rstd[:, k : k + 1], -1.0, ALU.mult, ALU.mult
-                    )
-                    normed_block = norm.tile([P, C], F32, name="normed_block")
-                    nc.scalar.activation(
-                        normed_block[:], words[k][:], FUNC.Identity, bias=shift[:], scale=rstd[:, k : k + 1]
-                    )
-                    normed.append(normed_block)
-
-            for b in range(CHANNEL_BLOCKS):
-                e_bank = back.tile([P, BANK], F32, name="e_bank")
-                for i, normed_block in enumerate(normed):
+        for b in range(CHANNEL_BLOCKS):
+            e = held.tile([P, S], F32, name=f"e{b}")
+            for g in range(GROUPS):
+                e_bank = psum.tile([P, BANK], F32, name="bank")
+                for i in range(BLOCKS_IN_GROUP):
                     nc.tensor.transpose(
                         e_bank[:, i * P : (i + 1) * P],
-                        normed_block[:, b * P : (b + 1) * P],
+                        normed[g * BLOCKS_IN_GROUP + i][:, b * P : (b + 1) * P],
                         identity[:],
                     )
-                if b % 2 == 0:
-                    nc.scalar.copy(e[b][:, g * BANK : (g + 1) * BANK], e_bank[:])
+                if g < GROUPS - 1:
+                    nc.scalar.copy(e[:, g * BANK : (g + 1) * BANK], e_bank[:])
                 else:
-                    nc.vector.tensor_copy(e[b][:, g * BANK : (g + 1) * BANK], e_bank[:])
+                    nc.vector.tensor_copy(e[:, g * BANK : (g + 1) * BANK], e_bank[:])
 
-        for b in range(CHANNEL_BLOCKS):
             picked = rows.tile([P, N], F32, name="picked")
-            nc.vector.tensor_tensor(picked[:], e[b][:].indirect(offsets[:]), minus_avg_row[b][:], ALU.add)
+            nc.vector.tensor_tensor(picked[:], e[:].indirect(offsets[:]), minus_avg_row[b][:], ALU.add)
             nc.sync.dma_start(out[b * P : (b + 1) * P, :], picked[:])

@@ -42,8 +42,19 @@ def tile_gdw_kernel(tc, wte, offs, out):
         eps = held.tile([P, 1], F32, name="eps")
         nc.vector.memset(eps[:], EPS)
 
+        added = [
+            [held.tile([P, BANK], F32, name=f"added{h}_{b}") for b in range(CHANNEL_BLOCKS)] for h in range(2)
+        ]
+        for h in range(2):
+            for b in range(CHANNEL_BLOCKS):
+                nc.gpsimd.tensor_add(
+                    added[h][b][:],
+                    raw[b][:, 2 * h * BANK : (2 * h + 1) * BANK],
+                    raw[b][:, (2 * h + 1) * BANK : (2 * h + 2) * BANK],
+                )
+
         normed = [held.tile([P, C], F32, name=f"normed{j}") for j in range(2 * PAIRS)]
-        minus_avg_parts = held.tile([P, CHANNEL_BLOCKS, GROUPS], F32, name="minus_avg_parts")
+        minus_avg_parts = held.tile([P, CHANNEL_BLOCKS, 2], F32, name="minus_avg_parts")
         flipped, mean_var, std, rstd, shift = {}, {}, {}, {}, {}
 
         def flip_pair(p):
@@ -71,41 +82,32 @@ def tile_gdw_kernel(tc, wte, offs, out):
         def invert_pair(p):
             rstd[p] = small.tile([P, 2], F32, name="rstd")
             nc.vector.reciprocal(rstd[p][:], std[p][:])
-            shift[p] = small.tile([P, 1], F32, name="shift")
-            nc.vector.tensor_scalar(
-                shift[p][:], mean_var[p][:, 0, 0:1], rstd[p][:, 0:1], -1.0, ALU.mult, ALU.mult
-            )
+            shift[p] = small.tile([P, 2], F32, name="shift")
+            for k in range(2):
+                nc.vector.tensor_scalar(
+                    shift[p][:, k : k + 1], mean_var[p][:, k, 0:1], rstd[p][:, k : k + 1], -1.0, ALU.mult, ALU.mult
+                )
 
         def normalise_pair(p):
-            nc.scalar.activation(
-                normed[2 * p][:], flipped[p][0][:], FUNC.Identity, bias=shift[p][:], scale=rstd[p][:, 0:1]
-            )
-            nc.vector.tensor_scalar(
-                normed[2 * p + 1][:],
-                flipped[p][1][:],
-                mean_var[p][:, 1, 0:1],
-                rstd[p][:, 1:2],
-                ALU.subtract,
-                ALU.mult,
-            )
-
-        def sum_rows(p):
-            g = p // 2
-            for b in (2 * (p % 2), 2 * (p % 2) + 1):
-                scaled = rows.tile([P, BANK], F32, name="scaled")
+            for k in range(2):
                 nc.scalar.activation(
-                    scaled[:],
-                    raw[b][:, g * BANK : (g + 1) * BANK],
-                    FUNC.Copy,
-                    scale=-1.0 / S,
-                    accum_out=minus_avg_parts[:, b, g : g + 1],
+                    normed[2 * p + k][:],
+                    flipped[p][k][:],
+                    FUNC.Identity,
+                    bias=shift[p][:, k : k + 1],
+                    scale=rstd[p][:, k : k + 1],
                 )
+
+        def sum_added(n):
+            h, b = divmod(n, CHANNEL_BLOCKS)
+            scaled = rows.tile([P, BANK], F32, name="scaled")
+            nc.scalar.activation(
+                scaled[:], added[h][b][:], FUNC.Copy, scale=-1.0 / S, accum_out=minus_avg_parts[:, b, h : h + 1]
+            )
 
         flip_pair(0)
         flip_pair(1)
         flip_pair(2)
-        sum_rows(0)
-        sum_rows(1)
         measure_pair(0)
         root_pair(0)
         measure_pair(1)
@@ -115,12 +117,15 @@ def tile_gdw_kernel(tc, wte, offs, out):
             if p + 3 < PAIRS:
                 flip_pair(p + 3)
             normalise_pair(p)
+            if p >= 2:
+                sum_added(p - 2)
             if p + 2 < PAIRS:
-                sum_rows(p + 2)
                 measure_pair(p + 2)
                 root_pair(p + 2)
             if p + 1 < PAIRS:
                 invert_pair(p + 1)
+        sum_added(PAIRS - 2)
+        sum_added(PAIRS - 1)
 
         minus_avg = held.tile([P, CHANNEL_BLOCKS], F32, name="minus_avg")
         nc.vector.reduce_sum(minus_avg[:], minus_avg_parts[:], axis=AXIS.X)

@@ -42,16 +42,11 @@ def tile_gdw_kernel(tc, wte, offs, out):
         eps = held.tile([P, 1], F32, name="eps")
         nc.vector.memset(eps[:], EPS)
 
-        added = [
-            [held.tile([P, BANK], F32, name=f"added{h}_{b}") for b in range(CHANNEL_BLOCKS)] for h in range(2)
-        ]
-        for h in range(2):
-            for b in range(CHANNEL_BLOCKS):
-                nc.gpsimd.tensor_add(
-                    added[h][b][:],
-                    raw[b][:, 2 * h * BANK : (2 * h + 1) * BANK],
-                    raw[b][:, (2 * h + 1) * BANK : (2 * h + 2) * BANK],
-                )
+        added = [held.tile([P, BANK], F32, name=f"added{b}") for b in range(CHANNEL_BLOCKS)]
+        for b in range(CHANNEL_BLOCKS):
+            nc.gpsimd.tensor_add(added[b][:], raw[b][:, BANK : 2 * BANK], raw[b][:, 2 * BANK : 3 * BANK])
+        for b in range(CHANNEL_BLOCKS):
+            nc.gpsimd.tensor_add(added[b][:], added[b][:], raw[b][:, 3 * BANK : 4 * BANK])
 
         normed = [held.tile([P, C], F32, name=f"normed{j}") for j in range(2 * PAIRS)]
         minus_avg_parts = held.tile([P, CHANNEL_BLOCKS, 2], F32, name="minus_avg_parts")
@@ -98,16 +93,17 @@ def tile_gdw_kernel(tc, wte, offs, out):
                     scale=rstd[p][:, k : k + 1],
                 )
 
-        def sum_added(n):
-            h, b = divmod(n, CHANNEL_BLOCKS)
+        def sum_row(words, b, part):
             scaled = rows.tile([P, BANK], F32, name="scaled")
             nc.scalar.activation(
-                scaled[:], added[h][b][:], FUNC.Copy, scale=-1.0 / S, accum_out=minus_avg_parts[:, b, h : h + 1]
+                scaled[:], words, FUNC.Copy, scale=-1.0 / S, accum_out=minus_avg_parts[:, b, part : part + 1]
             )
 
         flip_pair(0)
         flip_pair(1)
         flip_pair(2)
+        for b in range(CHANNEL_BLOCKS):
+            sum_row(raw[b][:, 0:BANK], b, 0)
         measure_pair(0)
         root_pair(0)
         measure_pair(1)
@@ -117,15 +113,14 @@ def tile_gdw_kernel(tc, wte, offs, out):
             if p + 3 < PAIRS:
                 flip_pair(p + 3)
             normalise_pair(p)
-            if p >= 2:
-                sum_added(p - 2)
+            if p >= PAIRS - CHANNEL_BLOCKS:
+                b = p - (PAIRS - CHANNEL_BLOCKS)
+                sum_row(added[b][:], b, 1)
             if p + 2 < PAIRS:
                 measure_pair(p + 2)
                 root_pair(p + 2)
             if p + 1 < PAIRS:
                 invert_pair(p + 1)
-        sum_added(PAIRS - 2)
-        sum_added(PAIRS - 1)
 
         minus_avg = held.tile([P, CHANNEL_BLOCKS], F32, name="minus_avg")
         nc.vector.reduce_sum(minus_avg[:], minus_avg_parts[:], axis=AXIS.X)

@@ -26,27 +26,30 @@ def tile_gdw_kernel(tc, wte, offs, out):
         tc.tile_pool(name="small", bufs=6) as small,
         tc.psum_pool(name="psum", bufs=PSUM_BANKS) as psum,
     ):
+        raw = [held.tile([P, S], F32, name=f"raw{b}") for b in range(CHANNEL_BLOCKS)]
+        load_edges = [0, BANK // 2] + [g * BANK for g in range(1, GROUPS + 1)]
+        for first, end in zip(load_edges[:-1], load_edges[1:]):
+            for b in range(CHANNEL_BLOCKS):
+                nc.sync.dma_start(raw[b][:, first:end], wte[b * P : (b + 1) * P, first:end])
+
         offsets = held.tile([P, N // 16], U16, name="offsets")
         nc.sync.dma_start(offsets[:], offs)
-
-        raw = [held.tile([P, S], F32, name=f"raw{b}") for b in range(CHANNEL_BLOCKS)]
-        for g in range(GROUPS):
-            for b in range(CHANNEL_BLOCKS):
-                nc.sync.dma_start(
-                    raw[b][:, g * BANK : (g + 1) * BANK],
-                    wte[b * P : (b + 1) * P, g * BANK : (g + 1) * BANK],
-                )
 
         identity = held.tile([P, P], F32, name="identity")
         make_identity(nc, identity[:])
         eps = held.tile([P, 1], F32, name="eps")
         nc.vector.memset(eps[:], EPS)
 
-        added = [held.tile([P, BANK], F32, name=f"added{b}") for b in range(CHANNEL_BLOCKS)]
-        for b in range(CHANNEL_BLOCKS):
-            nc.gpsimd.tensor_add(added[b][:], raw[b][:, BANK : 2 * BANK], raw[b][:, 2 * BANK : 3 * BANK])
-        for b in range(CHANNEL_BLOCKS):
-            nc.gpsimd.tensor_add(added[b][:], added[b][:], raw[b][:, 3 * BANK : 4 * BANK])
+        added = [
+            [held.tile([P, BANK], F32, name=f"added{h}_{b}") for b in range(CHANNEL_BLOCKS)] for h in range(2)
+        ]
+        for h in range(2):
+            for b in range(CHANNEL_BLOCKS):
+                nc.gpsimd.tensor_add(
+                    added[h][b][:],
+                    raw[b][:, 2 * h * BANK : (2 * h + 1) * BANK],
+                    raw[b][:, (2 * h + 1) * BANK : (2 * h + 2) * BANK],
+                )
 
         normed = [held.tile([P, C], F32, name=f"normed{j}") for j in range(2 * PAIRS)]
         minus_avg_parts = held.tile([P, CHANNEL_BLOCKS, 2], F32, name="minus_avg_parts")
@@ -93,17 +96,16 @@ def tile_gdw_kernel(tc, wte, offs, out):
                     scale=rstd[p][:, k : k + 1],
                 )
 
-        def sum_row(words, b, part):
+        def sum_added(n):
+            h, b = divmod(n, CHANNEL_BLOCKS)
             scaled = rows.tile([P, BANK], F32, name="scaled")
             nc.scalar.activation(
-                scaled[:], words, FUNC.Copy, scale=-1.0 / S, accum_out=minus_avg_parts[:, b, part : part + 1]
+                scaled[:], added[h][b][:], FUNC.Copy, scale=-1.0 / S, accum_out=minus_avg_parts[:, b, h : h + 1]
             )
 
         flip_pair(0)
         flip_pair(1)
         flip_pair(2)
-        for b in range(CHANNEL_BLOCKS):
-            sum_row(raw[b][:, 0:BANK], b, 0)
         measure_pair(0)
         root_pair(0)
         measure_pair(1)
@@ -113,14 +115,15 @@ def tile_gdw_kernel(tc, wte, offs, out):
             if p + 3 < PAIRS:
                 flip_pair(p + 3)
             normalise_pair(p)
-            if p >= PAIRS - CHANNEL_BLOCKS:
-                b = p - (PAIRS - CHANNEL_BLOCKS)
-                sum_row(added[b][:], b, 1)
+            if p >= 2:
+                sum_added(p - 2)
             if p + 2 < PAIRS:
                 measure_pair(p + 2)
                 root_pair(p + 2)
             if p + 1 < PAIRS:
                 invert_pair(p + 1)
+        sum_added(PAIRS - 2)
+        sum_added(PAIRS - 1)
 
         minus_avg = held.tile([P, CHANNEL_BLOCKS], F32, name="minus_avg")
         nc.vector.reduce_sum(minus_avg[:], minus_avg_parts[:], axis=AXIS.X)
@@ -130,21 +133,31 @@ def tile_gdw_kernel(tc, wte, offs, out):
             nc.vector.tensor_copy(spread[:], minus_avg[:, b : b + 1].to_broadcast([P, N]))
             minus_avg_row.append(spread)
 
+        e = [held.tile([P, S], F32, name=f"e{b}") for b in range(CHANNEL_BLOCKS)]
+        LAST = GROUPS - 1
+
+        def flip_back(b, g, copy):
+            e_bank = psum.tile([P, BANK], F32, name="bank")
+            for i in range(BLOCKS_IN_GROUP):
+                nc.tensor.transpose(
+                    e_bank[:, i * P : (i + 1) * P],
+                    normed[g * BLOCKS_IN_GROUP + i][:, b * P : (b + 1) * P],
+                    identity[:],
+                )
+            copy(e[b][:, g * BANK : (g + 1) * BANK], e_bank[:])
+
+        for b in range(2):
+            for g in range(LAST):
+                flip_back(b, g, nc.vector.tensor_copy)
+
         for b in range(CHANNEL_BLOCKS):
-            e = held.tile([P, S], F32, name=f"e{b}")
-            for g in range(GROUPS):
-                e_bank = psum.tile([P, BANK], F32, name="bank")
-                for i in range(BLOCKS_IN_GROUP):
-                    nc.tensor.transpose(
-                        e_bank[:, i * P : (i + 1) * P],
-                        normed[g * BLOCKS_IN_GROUP + i][:, b * P : (b + 1) * P],
-                        identity[:],
-                    )
-                if g < GROUPS - 1:
-                    nc.scalar.copy(e[:, g * BANK : (g + 1) * BANK], e_bank[:])
-                else:
-                    nc.vector.tensor_copy(e[:, g * BANK : (g + 1) * BANK], e_bank[:])
+            if b < 2:
+                flip_back(b, LAST, nc.scalar.copy)
+            else:
+                for g in range(LAST):
+                    flip_back(b, g, nc.scalar.copy)
+                flip_back(b, LAST, nc.vector.tensor_copy)
 
             picked = rows.tile([P, N], F32, name="picked")
-            nc.vector.tensor_tensor(picked[:], e[:].indirect(offsets[:]), minus_avg_row[b][:], ALU.add)
+            nc.vector.tensor_tensor(picked[:], e[b][:].indirect(offsets[:]), minus_avg_row[b][:], ALU.add)
             nc.sync.dma_start(out[b * P : (b + 1) * P, :], picked[:])

@@ -5,7 +5,6 @@ F32 = mybir.dt.float32
 U16 = mybir.dt.uint16
 FUNC = mybir.ActivationFunctionType
 ALU = mybir.AluOpType
-AXIS = mybir.AxisListType
 
 P = 128
 C, S, N = 512, 2048, 512
@@ -39,6 +38,8 @@ def tile_gdw_kernel(tc, wte, offs, out):
         make_identity(nc, identity[:])
         eps = held.tile([P, 1], F32, name="eps")
         nc.vector.memset(eps[:], EPS)
+        ones = held.tile([P, N], F32, name="ones")
+        nc.vector.memset(ones[:], 1.0)
 
         added = [
             [held.tile([P, BANK], F32, name=f"added{h}_{b}") for b in range(CHANNEL_BLOCKS)] for h in range(2)
@@ -53,7 +54,7 @@ def tile_gdw_kernel(tc, wte, offs, out):
 
         normed = [held.tile([P, C], F32, name=f"normed{j}") for j in range(2 * PAIRS)]
         minus_avg_parts = held.tile([P, CHANNEL_BLOCKS, 2], F32, name="minus_avg_parts")
-        flipped, mean_var, std, rstd, shift = {}, {}, {}, {}, {}
+        flipped, mean_var, rstd, shift = {}, {}, {}, {}
 
         def flip_pair(p):
             flipped[p] = []
@@ -74,17 +75,14 @@ def tile_gdw_kernel(tc, wte, offs, out):
                 nc.vector.bn_aggr(mean_var[p][:, k, :], stats[:])
 
         def root_pair(p):
-            std[p] = small.tile([P, 2], F32, name="std")
-            nc.scalar.activation(std[p][:], mean_var[p][:, :, 1], FUNC.Sqrt, bias=eps[:])
+            rstd[p] = small.tile([P, 2], F32, name="rstd")
+            nc.scalar.activation(rstd[p][:], mean_var[p][:, :, 1], FUNC.Abs_reciprocal_sqrt, bias=eps[:])
 
         def invert_pair(p):
-            rstd[p] = small.tile([P, 2], F32, name="rstd")
-            nc.vector.reciprocal(rstd[p][:], std[p][:])
             shift[p] = small.tile([P, 2], F32, name="shift")
-            for k in range(2):
-                nc.vector.tensor_scalar(
-                    shift[p][:, k : k + 1], mean_var[p][:, k, 0:1], rstd[p][:, k : k + 1], -1.0, ALU.mult, ALU.mult
-                )
+            nc.vector.scalar_tensor_tensor(
+                shift[p][:], mean_var[p][:, :, 0], -1.0, rstd[p][:], ALU.mult, ALU.mult
+            )
 
         def normalise_pair(p):
             for k in range(2):
@@ -125,12 +123,12 @@ def tile_gdw_kernel(tc, wte, offs, out):
         sum_added(PAIRS - 2)
         sum_added(PAIRS - 1)
 
-        minus_avg = held.tile([P, CHANNEL_BLOCKS], F32, name="minus_avg")
-        nc.vector.reduce_sum(minus_avg[:], minus_avg_parts[:], axis=AXIS.X)
         minus_avg_row = []
         for b in range(CHANNEL_BLOCKS):
             spread = rows.tile([P, N], F32, name="spread")
-            nc.vector.tensor_copy(spread[:], minus_avg[:, b : b + 1].to_broadcast([P, N]))
+            nc.gpsimd.tensor_scalar(
+                spread[:], ones[:], minus_avg_parts[:, b, 0:1], minus_avg_parts[:, b, 1:2], ALU.mult, ALU.add
+            )
             minus_avg_row.append(spread)
 
         e = [held.tile([P, S], F32, name=f"e{b}") for b in range(CHANNEL_BLOCKS)]

@@ -22,14 +22,14 @@ def tile_gdw_kernel(tc, wte, offs, out):
     with (
         tc.tile_pool(name="held", bufs=1) as held,
         tc.tile_pool(name="rows", bufs=4) as rows,
-        tc.tile_pool(name="small", bufs=6) as small,
+        tc.tile_pool(name="small", bufs=4) as small,
         tc.psum_pool(name="psum", bufs=PSUM_BANKS) as psum,
     ):
-        raw = [held.tile([P, S], F32, name=f"raw{b}") for b in range(CHANNEL_BLOCKS)]
+        raw = held.tile([P, CHANNEL_BLOCKS, S], F32, name="raw")
         load_edges = [0, BANK // 2] + [g * BANK for g in range(1, GROUPS + 1)]
         for first, end in zip(load_edges[:-1], load_edges[1:]):
             for b in range(CHANNEL_BLOCKS):
-                nc.sync.dma_start(raw[b][:, first:end], wte[b * P : (b + 1) * P, first:end])
+                nc.sync.dma_start(raw[:, b, first:end], wte[b * P : (b + 1) * P, first:end])
 
         offsets = held.tile([P, N // 16], U16, name="offsets")
         nc.sync.dma_start(offsets[:], offs)
@@ -48,91 +48,75 @@ def tile_gdw_kernel(tc, wte, offs, out):
             for b in range(CHANNEL_BLOCKS):
                 nc.gpsimd.tensor_add(
                     added[h][b][:],
-                    raw[b][:, 2 * h * BANK : (2 * h + 1) * BANK],
-                    raw[b][:, (2 * h + 1) * BANK : (2 * h + 2) * BANK],
+                    raw[:, b, 2 * h * BANK : (2 * h + 1) * BANK],
+                    raw[:, b, (2 * h + 1) * BANK : (2 * h + 2) * BANK],
                 )
 
         normed = [held.tile([P, C], F32, name=f"normed{j}") for j in range(2 * PAIRS)]
-        minus_avg_parts = held.tile([P, CHANNEL_BLOCKS, 2], F32, name="minus_avg_parts")
         flipped, mean_var, rstd, shift = {}, {}, {}, {}
 
         def flip_pair(p):
-            flipped[p] = []
-            for k in range(2):
-                first_word = (2 * p + k) * P
-                block = psum.tile([P, C], F32, name="bank")
+            for j in (2 * p, 2 * p + 1):
+                flipped[j] = psum.tile([P, C], F32, name="bank")
                 for b in range(CHANNEL_BLOCKS):
                     nc.tensor.transpose(
-                        block[:, b * P : (b + 1) * P], raw[b][:, first_word : first_word + P], identity[:]
+                        flipped[j][:, b * P : (b + 1) * P], raw[:, b, j * P : (j + 1) * P], identity[:]
                     )
-                flipped[p].append(block)
 
-        def measure_pair(p):
-            mean_var[p] = small.tile([P, 2, 2], F32, name="mean_var")
-            for k in range(2):
-                stats = small.tile([P, 6], F32, name="stats")
-                nc.vector.bn_stats(stats[:], flipped[p][k][:])
-                nc.vector.bn_aggr(mean_var[p][:, k, :], stats[:])
+        def measure_block(p, k):
+            if k == 0:
+                mean_var[p] = small.tile([P, 2, 2], F32, name="mean_var")
+            stats = small.tile([P, 6], F32, name="stats")
+            nc.vector.bn_stats(stats[:], flipped[2 * p + k][:])
+            nc.vector.bn_aggr(mean_var[p][:, k, :], stats[:])
 
         def root_pair(p):
             rstd[p] = small.tile([P, 2], F32, name="rstd")
             nc.scalar.activation(rstd[p][:], mean_var[p][:, :, 1], FUNC.Abs_reciprocal_sqrt, bias=eps[:])
 
-        def invert_pair(p):
+        def shift_pair(p):
             shift[p] = small.tile([P, 2], F32, name="shift")
             nc.vector.scalar_tensor_tensor(
                 shift[p][:], mean_var[p][:, :, 0], -1.0, rstd[p][:], ALU.mult, ALU.mult
             )
 
-        def normalise_pair(p):
+        def normalise_pair_on_scalar(p):
             for k in range(2):
                 nc.scalar.activation(
                     normed[2 * p + k][:],
-                    flipped[p][k][:],
+                    flipped[2 * p + k][:],
                     FUNC.Identity,
                     bias=shift[p][:, k : k + 1],
                     scale=rstd[p][:, k : k + 1],
                 )
 
-        def sum_added(n):
-            h, b = divmod(n, CHANNEL_BLOCKS)
-            scaled = rows.tile([P, BANK], F32, name="scaled")
-            nc.scalar.activation(
-                scaled[:], added[h][b][:], FUNC.Copy, scale=-1.0 / S, accum_out=minus_avg_parts[:, b, h : h + 1]
-            )
+        def normalise_pair_on_vector(p):
+            for k in range(2):
+                nc.vector.tensor_scalar(
+                    normed[2 * p + k][:],
+                    flipped[2 * p + k][:],
+                    mean_var[p][:, k, 0:1],
+                    rstd[p][:, k : k + 1],
+                    ALU.subtract,
+                    ALU.mult,
+                )
 
         flip_pair(0)
         flip_pair(1)
-        flip_pair(2)
-        measure_pair(0)
+        measure_block(0, 0)
+        measure_block(0, 1)
         root_pair(0)
-        measure_pair(1)
-        root_pair(1)
-        invert_pair(0)
-        for p in range(PAIRS):
-            if p + 3 < PAIRS:
-                flip_pair(p + 3)
-            normalise_pair(p)
-            if p >= 2:
-                sum_added(p - 2)
+        for p in range(PAIRS - 1):
             if p + 2 < PAIRS:
-                measure_pair(p + 2)
-                root_pair(p + 2)
-            if p + 1 < PAIRS:
-                invert_pair(p + 1)
-        sum_added(PAIRS - 2)
-        sum_added(PAIRS - 1)
-
-        minus_avg_row = []
-        for b in range(CHANNEL_BLOCKS):
-            spread = rows.tile([P, N], F32, name="spread")
-            nc.gpsimd.tensor_scalar(
-                spread[:], ones[:], minus_avg_parts[:, b, 0:1], minus_avg_parts[:, b, 1:2], ALU.mult, ALU.add
-            )
-            minus_avg_row.append(spread)
+                flip_pair(p + 2)
+            measure_block(p + 1, 0)
+            shift_pair(p)
+            measure_block(p + 1, 1)
+            root_pair(p + 1)
+            normalise_pair_on_scalar(p)
+        normalise_pair_on_vector(PAIRS - 1)
 
         e = [held.tile([P, S], F32, name=f"e{b}") for b in range(CHANNEL_BLOCKS)]
-        LAST = GROUPS - 1
 
         def flip_back(b, g, copy):
             e_bank = psum.tile([P, BANK], F32, name="bank")
@@ -144,18 +128,37 @@ def tile_gdw_kernel(tc, wte, offs, out):
                 )
             copy(e[b][:, g * BANK : (g + 1) * BANK], e_bank[:])
 
-        for b in range(2):
-            for g in range(LAST):
-                flip_back(b, g, nc.vector.tensor_copy)
+        minus_avg_parts = held.tile([P, CHANNEL_BLOCKS, 2], F32, name="minus_avg_parts")
+        minus_avg_row = []
 
-        for b in range(CHANNEL_BLOCKS):
-            if b < 2:
-                flip_back(b, LAST, nc.scalar.copy)
-            else:
-                for g in range(LAST):
-                    flip_back(b, g, nc.scalar.copy)
-                flip_back(b, LAST, nc.vector.tensor_copy)
+        def spread_minus_avg(b):
+            for h in range(2):
+                scaled = rows.tile([P, BANK], F32, name="scaled")
+                nc.scalar.activation(
+                    scaled[:], added[h][b][:], FUNC.Copy, scale=-1.0 / S, accum_out=minus_avg_parts[:, b, h : h + 1]
+                )
+            spread = rows.tile([P, N], F32, name="spread")
+            nc.gpsimd.tensor_scalar(
+                spread[:], ones[:], minus_avg_parts[:, b, 0:1], minus_avg_parts[:, b, 1:2], ALU.mult, ALU.add
+            )
+            minus_avg_row.append(spread)
 
+        def look_up(b):
             picked = rows.tile([P, N], F32, name="picked")
             nc.vector.tensor_tensor(picked[:], e[b][:].indirect(offsets[:]), minus_avg_row[b][:], ALU.add)
             nc.sync.dma_start(out[b * P : (b + 1) * P, :], picked[:])
+
+        for b in range(2):
+            for g in range(GROUPS):
+                flip_back(b, g, nc.vector.tensor_copy)
+        flip_back(2, 0, nc.vector.tensor_copy)
+        for b in range(CHANNEL_BLOCKS):
+            spread_minus_avg(b)
+        for g in range(1, GROUPS):
+            flip_back(2, g, nc.scalar.copy)
+        look_up(0)
+        look_up(1)
+        for g in range(GROUPS):
+            flip_back(3, g, nc.scalar.copy)
+        look_up(2)
+        look_up(3)

@@ -22,7 +22,7 @@ def tile_gdw_kernel(tc, wte, offs, out):
     with (
         tc.tile_pool(name="held", bufs=1) as held,
         tc.tile_pool(name="rows", bufs=4) as rows,
-        tc.tile_pool(name="small", bufs=4) as small,
+        tc.tile_pool(name="small", bufs=6) as small,
         tc.psum_pool(name="psum", bufs=PSUM_BANKS) as psum,
     ):
         raw = held.tile([P, CHANNEL_BLOCKS, S], F32, name="raw")
@@ -53,7 +53,7 @@ def tile_gdw_kernel(tc, wte, offs, out):
                 )
 
         normed = [held.tile([P, C], F32, name=f"normed{j}") for j in range(2 * PAIRS)]
-        flipped, mean_var, rstd, shift = {}, {}, {}, {}
+        flipped, stats, mean_var, rstd, shift = {}, {}, {}, {}, {}
 
         def flip_pair(p):
             for j in (2 * p, 2 * p + 1):
@@ -63,12 +63,15 @@ def tile_gdw_kernel(tc, wte, offs, out):
                         flipped[j][:, b * P : (b + 1) * P], raw[:, b, j * P : (j + 1) * P], identity[:]
                     )
 
-        def measure_block(p, k):
+        def measure_block(j):
+            stats[j] = small.tile([P, 6], F32, name="stats")
+            nc.vector.bn_stats(stats[j][:], flipped[j][:])
+
+        def aggregate_block(j):
+            p, k = divmod(j, 2)
             if k == 0:
                 mean_var[p] = small.tile([P, 2, 2], F32, name="mean_var")
-            stats = small.tile([P, 6], F32, name="stats")
-            nc.vector.bn_stats(stats[:], flipped[2 * p + k][:])
-            nc.vector.bn_aggr(mean_var[p][:, k, :], stats[:])
+            nc.vector.bn_aggr(mean_var[p][:, k, :], stats[j][:])
 
         def root_pair(p):
             rstd[p] = small.tile([P, 2], F32, name="rstd")
@@ -80,15 +83,15 @@ def tile_gdw_kernel(tc, wte, offs, out):
                 shift[p][:], mean_var[p][:, :, 0], -1.0, rstd[p][:], ALU.mult, ALU.mult
             )
 
-        def normalise_pair_on_scalar(p):
-            for k in range(2):
-                nc.scalar.activation(
-                    normed[2 * p + k][:],
-                    flipped[2 * p + k][:],
-                    FUNC.Identity,
-                    bias=shift[p][:, k : k + 1],
-                    scale=rstd[p][:, k : k + 1],
-                )
+        def normalise_block_on_scalar(j):
+            p, k = divmod(j, 2)
+            nc.scalar.activation(
+                normed[j][:],
+                flipped[j][:],
+                FUNC.Identity,
+                bias=shift[p][:, k : k + 1],
+                scale=rstd[p][:, k : k + 1],
+            )
 
         def normalise_pair_on_vector(p):
             for k in range(2):
@@ -103,17 +106,25 @@ def tile_gdw_kernel(tc, wte, offs, out):
 
         flip_pair(0)
         flip_pair(1)
-        measure_block(0, 0)
-        measure_block(0, 1)
-        root_pair(0)
-        for p in range(PAIRS - 1):
-            if p + 2 < PAIRS:
-                flip_pair(p + 2)
-            measure_block(p + 1, 0)
-            shift_pair(p)
-            measure_block(p + 1, 1)
-            root_pair(p + 1)
-            normalise_pair_on_scalar(p)
+        flip_pair(2)
+        measure_block(0)
+        measure_block(1)
+        aggregate_block(0)
+        for p in range(PAIRS):
+            last = p == PAIRS - 1
+            if p + 3 < PAIRS:
+                flip_pair(p + 3)
+            if not last:
+                measure_block(2 * p + 2)
+            aggregate_block(2 * p + 1)
+            root_pair(p)
+            if p > 0:
+                normalise_block_on_scalar(2 * p - 1)
+            if not last:
+                measure_block(2 * p + 3)
+                aggregate_block(2 * p + 2)
+                shift_pair(p)
+                normalise_block_on_scalar(2 * p)
         normalise_pair_on_vector(PAIRS - 1)
 
         e = [held.tile([P, S], F32, name=f"e{b}") for b in range(CHANNEL_BLOCKS)]

@@ -14,7 +14,9 @@ PSUM_BANKS = 8
 CHANNEL_BLOCKS = C // P
 GROUPS = S // BANK
 BLOCKS_IN_GROUP = BANK // P
-PAIRS = S // (2 * P)
+BLOCKS = S // P
+PAIRS = BLOCKS // 2
+FLIP_AHEAD = 3
 
 
 def tile_gdw_kernel(tc, wte, offs, out):
@@ -52,16 +54,13 @@ def tile_gdw_kernel(tc, wte, offs, out):
                     raw[:, b, (2 * h + 1) * BANK : (2 * h + 2) * BANK],
                 )
 
-        normed = [held.tile([P, C], F32, name=f"normed{j}") for j in range(2 * PAIRS)]
+        normed = [held.tile([P, C], F32, name=f"normed{j}") for j in range(BLOCKS)]
         flipped, stats, mean_var, rstd, shift = {}, {}, {}, {}, {}
 
-        def flip_pair(p):
-            for j in (2 * p, 2 * p + 1):
-                flipped[j] = psum.tile([P, C], F32, name="bank")
-                for b in range(CHANNEL_BLOCKS):
-                    nc.tensor.transpose(
-                        flipped[j][:, b * P : (b + 1) * P], raw[:, b, j * P : (j + 1) * P], identity[:]
-                    )
+        def flip_block(j):
+            flipped[j] = psum.tile([P, C], F32, name="bank")
+            for b in range(CHANNEL_BLOCKS):
+                nc.tensor.transpose(flipped[j][:, b * P : (b + 1) * P], raw[:, b, j * P : (j + 1) * P], identity[:])
 
         def measure_block(j):
             stats[j] = small.tile([P, 6], F32, name="stats")
@@ -104,29 +103,6 @@ def tile_gdw_kernel(tc, wte, offs, out):
                     ALU.mult,
                 )
 
-        flip_pair(0)
-        flip_pair(1)
-        flip_pair(2)
-        measure_block(0)
-        measure_block(1)
-        aggregate_block(0)
-        for p in range(PAIRS):
-            last = p == PAIRS - 1
-            if p + 3 < PAIRS:
-                flip_pair(p + 3)
-            if not last:
-                measure_block(2 * p + 2)
-            aggregate_block(2 * p + 1)
-            root_pair(p)
-            if p > 0:
-                normalise_block_on_scalar(2 * p - 1)
-            if not last:
-                measure_block(2 * p + 3)
-                aggregate_block(2 * p + 2)
-                shift_pair(p)
-                normalise_block_on_scalar(2 * p)
-        normalise_pair_on_vector(PAIRS - 1)
-
         e = [held.tile([P, S], F32, name=f"e{b}") for b in range(CHANNEL_BLOCKS)]
 
         def flip_back(b, g, copy):
@@ -138,6 +114,26 @@ def tile_gdw_kernel(tc, wte, offs, out):
                     identity[:],
                 )
             copy(e[b][:, g * BANK : (g + 1) * BANK], e_bank[:])
+
+        for j in range(FLIP_AHEAD):
+            flip_block(j)
+        for j in range(BLOCKS + 1):
+            if j + FLIP_AHEAD < BLOCKS:
+                flip_block(j + FLIP_AHEAD)
+            if j < BLOCKS:
+                measure_block(j)
+            if j >= 1:
+                aggregate_block(j - 1)
+            if j >= 2 and j % 2 == 0:
+                root_pair(j // 2 - 1)
+            if j >= 4 and j % 2 == 0:
+                shift_pair(j // 2 - 2)
+            if j >= 4:
+                normalise_block_on_scalar(j - 4)
+        flip_back(0, 0, nc.vector.tensor_copy)
+        normalise_block_on_scalar(BLOCKS - 3)
+        flip_back(0, 1, nc.vector.tensor_copy)
+        normalise_pair_on_vector(PAIRS - 1)
 
         minus_avg_parts = held.tile([P, CHANNEL_BLOCKS, 2], F32, name="minus_avg_parts")
         minus_avg_row = []
@@ -159,9 +155,10 @@ def tile_gdw_kernel(tc, wte, offs, out):
             nc.vector.tensor_tensor(picked[:], e[b][:].indirect(offsets[:]), minus_avg_row[b][:], ALU.add)
             nc.sync.dma_start(out[b * P : (b + 1) * P, :], picked[:])
 
-        for b in range(2):
-            for g in range(GROUPS):
-                flip_back(b, g, nc.vector.tensor_copy)
+        for g in range(2, GROUPS):
+            flip_back(0, g, nc.vector.tensor_copy)
+        for g in range(GROUPS):
+            flip_back(1, g, nc.vector.tensor_copy)
         flip_back(2, 0, nc.vector.tensor_copy)
         for b in range(CHANNEL_BLOCKS):
             spread_minus_avg(b)

@@ -53,6 +53,10 @@ def tile_gdw_kernel(tc, wte, offs, out):
                     raw[:, b, 2 * h * BANK : (2 * h + 1) * BANK],
                     raw[:, b, (2 * h + 1) * BANK : (2 * h + 2) * BANK],
                 )
+        added_again = {}
+        for b in range(CHANNEL_BLOCKS // 2, CHANNEL_BLOCKS):
+            added_again[b] = held.tile([P, BANK], F32, name=f"added_again{b}")
+            nc.gpsimd.tensor_add(added_again[b][:], added[0][b][:], added[1][b][:])
 
         normed = [held.tile([P, C], F32, name=f"normed{j}") for j in range(BLOCKS)]
         flipped, stats, mean_var, rstd, shift = {}, {}, {}, {}, {}
@@ -78,9 +82,17 @@ def tile_gdw_kernel(tc, wte, offs, out):
 
         def shift_pair(p):
             shift[p] = small.tile([P, 2], F32, name="shift")
-            nc.vector.scalar_tensor_tensor(
-                shift[p][:], mean_var[p][:, :, 0], -1.0, rstd[p][:], ALU.mult, ALU.mult
-            )
+            product = small.tile([P, 2], F32, name="product")
+            for k in range(2):
+                nc.vector.tensor_scalar(
+                    product[:, k : k + 1],
+                    mean_var[p][:, k, 0:1],
+                    rstd[p][:, k : k + 1],
+                    None,
+                    ALU.mult,
+                    ALU.subtract,
+                    accum_out=shift[p][:, k : k + 1],
+                )
 
         def normalise_block_on_scalar(j):
             p, k = divmod(j, 2)
@@ -139,15 +151,15 @@ def tile_gdw_kernel(tc, wte, offs, out):
         minus_avg_row = []
 
         def spread_minus_avg(b):
-            for h in range(2):
+            to_sum = [added_again[b]] if b in added_again else [added[0][b], added[1][b]]
+            for h, words in enumerate(to_sum):
                 scaled = rows.tile([P, BANK], F32, name="scaled")
                 nc.scalar.activation(
-                    scaled[:], added[h][b][:], FUNC.Copy, scale=-1.0 / S, accum_out=minus_avg_parts[:, b, h : h + 1]
+                    scaled[:], words[:], FUNC.Copy, scale=-1.0 / S, accum_out=minus_avg_parts[:, b, h : h + 1]
                 )
+            second_part = minus_avg_parts[:, b, 1:2] if len(to_sum) == 2 else 0.0
             spread = rows.tile([P, N], F32, name="spread")
-            nc.gpsimd.tensor_scalar(
-                spread[:], ones[:], minus_avg_parts[:, b, 0:1], minus_avg_parts[:, b, 1:2], ALU.mult, ALU.add
-            )
+            nc.gpsimd.tensor_scalar(spread[:], ones[:], minus_avg_parts[:, b, 0:1], second_part, ALU.mult, ALU.add)
             minus_avg_row.append(spread)
 
         def look_up(b):
@@ -155,14 +167,14 @@ def tile_gdw_kernel(tc, wte, offs, out):
             nc.vector.tensor_tensor(picked[:], e[b][:].indirect(offsets[:]), minus_avg_row[b][:], ALU.add)
             nc.sync.dma_start(out[b * P : (b + 1) * P, :], picked[:])
 
-        for g in range(2, GROUPS):
-            flip_back(0, g, nc.vector.tensor_copy)
-        for g in range(GROUPS):
+        flip_back(0, 2, nc.vector.tensor_copy)
+        for g in range(GROUPS - 1):
             flip_back(1, g, nc.vector.tensor_copy)
-        flip_back(2, 0, nc.vector.tensor_copy)
         for b in range(CHANNEL_BLOCKS):
             spread_minus_avg(b)
-        for g in range(1, GROUPS):
+        flip_back(0, GROUPS - 1, nc.vector.tensor_copy)
+        flip_back(1, GROUPS - 1, nc.scalar.copy)
+        for g in range(GROUPS):
             flip_back(2, g, nc.scalar.copy)
         look_up(0)
         look_up(1)

@@ -17,6 +17,7 @@ BLOCKS_IN_GROUP = BANK // P
 BLOCKS = S // P
 PAIRS = BLOCKS // 2
 FLIP_AHEAD = 3
+EARLY_SUM_STEPS = [9, 12]
 
 
 def tile_gdw_kernel(tc, wte, offs, out):
@@ -57,6 +58,14 @@ def tile_gdw_kernel(tc, wte, offs, out):
         for b in range(CHANNEL_BLOCKS // 2, CHANNEL_BLOCKS):
             added_again[b] = held.tile([P, BANK], F32, name=f"added_again{b}")
             nc.gpsimd.tensor_add(added_again[b][:], added[0][b][:], added[1][b][:])
+
+        minus_avg_parts = held.tile([P, CHANNEL_BLOCKS, 2], F32, name="minus_avg_parts")
+
+        def sum_words(b, part, words):
+            scaled = rows.tile([P, BANK], F32, name="scaled")
+            nc.scalar.activation(
+                scaled[:], words[:], FUNC.Copy, scale=-1.0 / S, accum_out=minus_avg_parts[:, b, part : part + 1]
+            )
 
         normed = [held.tile([P, C], F32, name=f"normed{j}") for j in range(BLOCKS)]
         flipped, stats, mean_var, rstd, shift = {}, {}, {}, {}, {}
@@ -142,22 +151,23 @@ def tile_gdw_kernel(tc, wte, offs, out):
                 shift_pair(j // 2 - 2)
             if j >= 4:
                 normalise_block_on_scalar(j - 4)
+            if j in EARLY_SUM_STEPS:
+                b = EARLY_SUM_STEPS.index(j)
+                sum_words(b, 0, added[0][b])
         flip_back(0, 0, nc.vector.tensor_copy)
         normalise_block_on_scalar(BLOCKS - 3)
         flip_back(0, 1, nc.vector.tensor_copy)
         normalise_pair_on_vector(PAIRS - 1)
 
-        minus_avg_parts = held.tile([P, CHANNEL_BLOCKS, 2], F32, name="minus_avg_parts")
         minus_avg_row = []
 
         def spread_minus_avg(b):
-            to_sum = [added_again[b]] if b in added_again else [added[0][b], added[1][b]]
-            for h, words in enumerate(to_sum):
-                scaled = rows.tile([P, BANK], F32, name="scaled")
-                nc.scalar.activation(
-                    scaled[:], words[:], FUNC.Copy, scale=-1.0 / S, accum_out=minus_avg_parts[:, b, h : h + 1]
-                )
-            second_part = minus_avg_parts[:, b, 1:2] if len(to_sum) == 2 else 0.0
+            if b in added_again:
+                sum_words(b, 0, added_again[b])
+                second_part = 0.0
+            else:
+                sum_words(b, 1, added[1][b])
+                second_part = minus_avg_parts[:, b, 1:2]
             spread = rows.tile([P, N], F32, name="spread")
             nc.gpsimd.tensor_scalar(spread[:], ones[:], minus_avg_parts[:, b, 0:1], second_part, ALU.mult, ALU.add)
             minus_avg_row.append(spread)
@@ -167,15 +177,18 @@ def tile_gdw_kernel(tc, wte, offs, out):
             nc.vector.tensor_tensor(picked[:], e[b][:].indirect(offsets[:]), minus_avg_row[b][:], ALU.add)
             nc.sync.dma_start(out[b * P : (b + 1) * P, :], picked[:])
 
-        flip_back(0, 2, nc.vector.tensor_copy)
-        for g in range(GROUPS - 1):
-            flip_back(1, g, nc.vector.tensor_copy)
         for b in range(CHANNEL_BLOCKS):
             spread_minus_avg(b)
+        flip_back(0, 2, nc.vector.tensor_copy)
+        flip_back(1, 2, nc.scalar.copy)
+        flip_back(1, 0, nc.vector.tensor_copy)
+        flip_back(2, 0, nc.scalar.copy)
+        flip_back(2, 1, nc.scalar.copy)
+        flip_back(2, 2, nc.scalar.copy)
         flip_back(0, GROUPS - 1, nc.vector.tensor_copy)
+        flip_back(1, 1, nc.vector.tensor_copy)
         flip_back(1, GROUPS - 1, nc.scalar.copy)
-        for g in range(GROUPS):
-            flip_back(2, g, nc.scalar.copy)
+        flip_back(2, GROUPS - 1, nc.scalar.copy)
         look_up(0)
         look_up(1)
         for g in range(GROUPS):

@@ -91,16 +91,9 @@ def tile_gdw_kernel(tc, wte, offs, out):
 
         def shift_pair(p):
             shift[p] = small.tile([P, 2], F32, name="shift")
-            product = small.tile([P, 2], F32, name="product")
             for k in range(2):
                 nc.vector.tensor_scalar(
-                    product[:, k : k + 1],
-                    mean_var[p][:, k, 0:1],
-                    rstd[p][:, k : k + 1],
-                    None,
-                    ALU.mult,
-                    ALU.subtract,
-                    accum_out=shift[p][:, k : k + 1],
+                    shift[p][:, k : k + 1], mean_var[p][:, k, 0:1], rstd[p][:, k : k + 1], -1.0, ALU.mult, ALU.mult
                 )
 
         def normalise_block_on_scalar(j):

@@ -17,7 +17,7 @@ BLOCKS_IN_GROUP = BANK // P
 BLOCKS = S // P
 PAIRS = BLOCKS // 2
 FLIP_AHEAD = 3
-EARLY_SUM_STEPS = [9, 12]
+EARLY_PIECES = 3
 
 
 def tile_gdw_kernel(tc, wte, offs, out):
@@ -41,31 +41,36 @@ def tile_gdw_kernel(tc, wte, offs, out):
         make_identity(nc, identity[:])
         eps = held.tile([P, 1], F32, name="eps")
         nc.vector.memset(eps[:], EPS)
+        unused = held.tile([P, 1], F32, name="unused")
+        nc.scalar.activation(unused[:], eps[:], FUNC.Abs_reciprocal_sqrt)
         ones = held.tile([P, N], F32, name="ones")
         nc.vector.memset(ones[:], 1.0)
 
-        added = [
-            [held.tile([P, BANK], F32, name=f"added{h}_{b}") for b in range(CHANNEL_BLOCKS)] for h in range(2)
-        ]
-        for h in range(2):
-            for b in range(CHANNEL_BLOCKS):
-                nc.gpsimd.tensor_add(
-                    added[h][b][:],
-                    raw[:, b, 2 * h * BANK : (2 * h + 1) * BANK],
-                    raw[:, b, (2 * h + 1) * BANK : (2 * h + 2) * BANK],
-                )
-        added_again = {}
-        for b in range(CHANNEL_BLOCKS // 2, CHANNEL_BLOCKS):
-            added_again[b] = held.tile([P, BANK], F32, name=f"added_again{b}")
-            nc.gpsimd.tensor_add(added_again[b][:], added[0][b][:], added[1][b][:])
+        early_sums = held.tile([P, EARLY_PIECES, CHANNEL_BLOCKS], F32, name="early_sums")
+        late_sums = held.tile([P, CHANNEL_BLOCKS], F32, name="late_sums")
 
-        minus_avg_parts = held.tile([P, CHANNEL_BLOCKS, 2], F32, name="minus_avg_parts")
-
-        def sum_words(b, part, words):
+        def sum_words(words, width, scale, total):
             scaled = rows.tile([P, BANK], F32, name="scaled")
-            nc.scalar.activation(
-                scaled[:], words[:], FUNC.Copy, scale=-1.0 / S, accum_out=minus_avg_parts[:, b, part : part + 1]
-            )
+            nc.scalar.activation(scaled[:, :width], words, FUNC.Copy, scale=scale, accum_out=total)
+
+        for k in range(EARLY_PIECES):
+            first, end = load_edges[k : k + 2]
+            for b in range(CHANNEL_BLOCKS):
+                sum_words(raw[:, b, first:end], end - first, -1.0 / S, early_sums[:, k, b : b + 1])
+
+        halves = []
+        for b in range(CHANNEL_BLOCKS):
+            added = held.tile([P, BANK], F32, name=f"added{b}")
+            nc.gpsimd.tensor_add(added[:], raw[:, b, 2 * BANK : 3 * BANK], raw[:, b, 3 * BANK : 4 * BANK])
+            halves.append(added)
+        for b in range(CHANNEL_BLOCKS):
+            half = held.tile([P, BANK // 2], F32, name=f"half{b}")
+            nc.gpsimd.tensor_add(half[:], halves[b][:, : BANK // 2], halves[b][:, BANK // 2 :])
+            halves[b] = half
+        early_sum = held.tile([P, CHANNEL_BLOCKS], F32, name="early_sum")
+        nc.gpsimd.tensor_add(early_sum[:], early_sums[:, 0, :], early_sums[:, 1, :])
+        early_total = held.tile([P, CHANNEL_BLOCKS], F32, name="early_total")
+        nc.gpsimd.tensor_add(early_total[:], early_sum[:], early_sums[:, 2, :])
 
         normed = [held.tile([P, C], F32, name=f"normed{j}") for j in range(BLOCKS)]
         flipped, stats, mean_var, rstd, shift = {}, {}, {}, {}, {}
@@ -89,33 +94,18 @@ def tile_gdw_kernel(tc, wte, offs, out):
             rstd[p] = small.tile([P, 2], F32, name="rstd")
             nc.scalar.activation(rstd[p][:], mean_var[p][:, :, 1], FUNC.Abs_reciprocal_sqrt, bias=eps[:])
 
-        def shift_pair(p):
-            shift[p] = small.tile([P, 2], F32, name="shift")
-            for k in range(2):
-                nc.vector.tensor_scalar(
-                    shift[p][:, k : k + 1], mean_var[p][:, k, 0:1], rstd[p][:, k : k + 1], -1.0, ALU.mult, ALU.mult
-                )
-
-        def normalise_block_on_scalar(j):
+        def shift_block(j):
             p, k = divmod(j, 2)
-            nc.scalar.activation(
-                normed[j][:],
-                flipped[j][:],
-                FUNC.Identity,
-                bias=shift[p][:, k : k + 1],
-                scale=rstd[p][:, k : k + 1],
+            shift[j] = small.tile([P, 1], F32, name="shift")
+            nc.vector.tensor_scalar(
+                shift[j][:], mean_var[p][:, k, 0:1], rstd[p][:, k : k + 1], -1.0, ALU.mult, ALU.mult
             )
 
-        def normalise_pair_on_vector(p):
-            for k in range(2):
-                nc.vector.tensor_scalar(
-                    normed[2 * p + k][:],
-                    flipped[2 * p + k][:],
-                    mean_var[p][:, k, 0:1],
-                    rstd[p][:, k : k + 1],
-                    ALU.subtract,
-                    ALU.mult,
-                )
+        def normalise_block(j):
+            p, k = divmod(j, 2)
+            nc.scalar.activation(
+                normed[j][:], flipped[j][:], FUNC.Identity, bias=shift[j][:], scale=rstd[p][:, k : k + 1]
+            )
 
         e = [held.tile([P, S], F32, name=f"e{b}") for b in range(CHANNEL_BLOCKS)]
 
@@ -131,38 +121,29 @@ def tile_gdw_kernel(tc, wte, offs, out):
 
         for j in range(FLIP_AHEAD):
             flip_block(j)
-        for j in range(BLOCKS + 1):
+        for j in range(BLOCKS + 4):
             if j + FLIP_AHEAD < BLOCKS:
                 flip_block(j + FLIP_AHEAD)
             if j < BLOCKS:
                 measure_block(j)
-            if j >= 1:
+            if 1 <= j <= BLOCKS:
                 aggregate_block(j - 1)
-            if j >= 2 and j % 2 == 0:
-                root_pair(j // 2 - 1)
-            if j >= 4 and j % 2 == 0:
-                shift_pair(j // 2 - 2)
+                if j % 2 == 0:
+                    root_pair(j // 2 - 1)
             if j >= 4:
-                normalise_block_on_scalar(j - 4)
-            if j in EARLY_SUM_STEPS:
-                b = EARLY_SUM_STEPS.index(j)
-                sum_words(b, 0, added[0][b])
-        flip_back(0, 0, nc.vector.tensor_copy)
-        normalise_block_on_scalar(BLOCKS - 3)
-        flip_back(0, 1, nc.vector.tensor_copy)
-        normalise_pair_on_vector(PAIRS - 1)
+                shift_block(j - 4)
+                normalise_block(j - 4)
 
+        late_scale = held.tile([P, 1], F32, name="late_scale")
+        nc.vector.tensor_scalar(late_scale[:], stats[BLOCKS - 1][:, 0:1], -1.0 / (S * (C // 2)), 0.0, ALU.mult, ALU.add)
         minus_avg_row = []
 
         def spread_minus_avg(b):
-            if b in added_again:
-                sum_words(b, 0, added_again[b])
-                second_part = 0.0
-            else:
-                sum_words(b, 1, added[1][b])
-                second_part = minus_avg_parts[:, b, 1:2]
+            sum_words(halves[b][:], BANK // 2, late_scale[:], late_sums[:, b : b + 1])
             spread = rows.tile([P, N], F32, name="spread")
-            nc.gpsimd.tensor_scalar(spread[:], ones[:], minus_avg_parts[:, b, 0:1], second_part, ALU.mult, ALU.add)
+            nc.gpsimd.tensor_scalar(
+                spread[:], ones[:], late_sums[:, b : b + 1], early_total[:, b : b + 1], ALU.mult, ALU.add
+            )
             minus_avg_row.append(spread)
 
         def look_up(b):
@@ -170,21 +151,24 @@ def tile_gdw_kernel(tc, wte, offs, out):
             nc.vector.tensor_tensor(picked[:], e[b][:].indirect(offsets[:]), minus_avg_row[b][:], ALU.add)
             nc.sync.dma_start(out[b * P : (b + 1) * P, :], picked[:])
 
-        for b in range(CHANNEL_BLOCKS):
-            spread_minus_avg(b)
-        flip_back(0, 2, nc.vector.tensor_copy)
-        flip_back(1, 2, nc.scalar.copy)
+        for g in range(GROUPS - 1):
+            flip_back(0, g, nc.vector.tensor_copy)
         flip_back(1, 0, nc.vector.tensor_copy)
-        flip_back(2, 0, nc.scalar.copy)
-        flip_back(2, 1, nc.scalar.copy)
-        flip_back(2, 2, nc.scalar.copy)
+        spread_minus_avg(0)
+        spread_minus_avg(1)
+        flip_back(1, 1, nc.scalar.copy)
+        flip_back(1, 2, nc.vector.tensor_copy)
+        flip_back(2, 0, nc.vector.tensor_copy)
         flip_back(0, GROUPS - 1, nc.vector.tensor_copy)
-        flip_back(1, 1, nc.vector.tensor_copy)
         flip_back(1, GROUPS - 1, nc.scalar.copy)
-        flip_back(2, GROUPS - 1, nc.scalar.copy)
         look_up(0)
+        spread_minus_avg(2)
+        spread_minus_avg(3)
+        for g in range(1, GROUPS):
+            flip_back(2, g, nc.scalar.copy)
         look_up(1)
-        for g in range(GROUPS):
+        flip_back(3, 0, nc.vector.tensor_copy)
+        for g in range(1, GROUPS):
             flip_back(3, g, nc.scalar.copy)
         look_up(2)
         look_up(3)

@@ -18,6 +18,7 @@ BLOCKS = S // P
 PAIRS = BLOCKS // 2
 FLIP_AHEAD = 3
 EARLY_PIECES = 3
+EARLY_BLOCKS = 3
 
 
 def tile_gdw_kernel(tc, wte, offs, out):
@@ -55,22 +56,25 @@ def tile_gdw_kernel(tc, wte, offs, out):
 
         for k in range(EARLY_PIECES):
             first, end = load_edges[k : k + 2]
-            for b in range(CHANNEL_BLOCKS):
+            for b in range(EARLY_BLOCKS if k == EARLY_PIECES - 1 else CHANNEL_BLOCKS):
                 sum_words(raw[:, b, first:end], end - first, -1.0 / S, early_sums[:, k, b : b + 1])
 
+        def add(x, y, width, name):
+            added = held.tile([P, width], F32, name=name)
+            nc.gpsimd.tensor_add(added[:], x, y)
+            return added
+
+        def group(b, g):
+            return raw[:, b, g * BANK : (g + 1) * BANK]
+
+        early_total = add(early_sums[:, 0, :], early_sums[:, 1, :], CHANNEL_BLOCKS, "early_total")
+        middle = {b: add(group(b, 1), group(b, 2), BANK, f"middle{b}") for b in range(EARLY_BLOCKS, CHANNEL_BLOCKS)}
         halves = []
         for b in range(CHANNEL_BLOCKS):
-            added = held.tile([P, BANK], F32, name=f"added{b}")
-            nc.gpsimd.tensor_add(added[:], raw[:, b, 2 * BANK : 3 * BANK], raw[:, b, 3 * BANK : 4 * BANK])
-            halves.append(added)
-        for b in range(CHANNEL_BLOCKS):
-            half = held.tile([P, BANK // 2], F32, name=f"half{b}")
-            nc.gpsimd.tensor_add(half[:], halves[b][:, : BANK // 2], halves[b][:, BANK // 2 :])
-            halves[b] = half
-        early_sum = held.tile([P, CHANNEL_BLOCKS], F32, name="early_sum")
-        nc.gpsimd.tensor_add(early_sum[:], early_sums[:, 0, :], early_sums[:, 1, :])
-        early_total = held.tile([P, CHANNEL_BLOCKS], F32, name="early_total")
-        nc.gpsimd.tensor_add(early_total[:], early_sum[:], early_sums[:, 2, :])
+            late = add(middle[b][:] if b in middle else group(b, 2), group(b, 3), BANK, f"late{b}")
+            halves.append(add(late[:, : BANK // 2], late[:, BANK // 2 :], BANK // 2, f"half{b}"))
+        third = early_sums[:, EARLY_PIECES - 1, :EARLY_BLOCKS]
+        nc.gpsimd.tensor_add(early_total[:, :EARLY_BLOCKS], early_total[:, :EARLY_BLOCKS], third)
 
         normed = [held.tile([P, C], F32, name=f"normed{j}") for j in range(BLOCKS)]
         flipped, stats, mean_var, rstd, shift = {}, {}, {}, {}, {}
@@ -146,10 +150,13 @@ def tile_gdw_kernel(tc, wte, offs, out):
             )
             minus_avg_row.append(spread)
 
-        def look_up(b):
-            picked = rows.tile([P, N], F32, name="picked")
-            nc.vector.tensor_tensor(picked[:], e[b][:].indirect(offsets[:]), minus_avg_row[b][:], ALU.add)
-            nc.sync.dma_start(out[b * P : (b + 1) * P, :], picked[:])
+        def look_up(b, pieces=1):
+            width = N // pieces
+            for first in range(0, N, width):
+                picked = rows.tile([P, width], F32, name="picked")
+                words = e[b][:].indirect(offsets[:, first // 16 : (first + width) // 16])
+                nc.vector.tensor_tensor(picked[:], words, minus_avg_row[b][:, first : first + width], ALU.add)
+                nc.sync.dma_start(out[b * P : (b + 1) * P, first : first + width], picked[:])
 
         for g in range(GROUPS - 1):
             flip_back(0, g, nc.vector.tensor_copy)
@@ -171,4 +178,4 @@ def tile_gdw_kernel(tc, wte, offs, out):
         for g in range(1, GROUPS):
             flip_back(3, g, nc.scalar.copy)
         look_up(2)
-        look_up(3)
+        look_up(3, pieces=2)

@@ -18,7 +18,7 @@ BLOCKS = S // P
 PAIRS = BLOCKS // 2
 FLIP_AHEAD = 3
 EARLY_PIECES = 3
-EARLY_BLOCKS = 3
+SKIPPED = 0
 
 
 def tile_gdw_kernel(tc, wte, offs, out):
@@ -31,8 +31,8 @@ def tile_gdw_kernel(tc, wte, offs, out):
     ):
         raw = held.tile([P, CHANNEL_BLOCKS, S], F32, name="raw")
         load_edges = [0, BANK // 2] + [g * BANK for g in range(1, GROUPS + 1)]
-        for first, end in zip(load_edges[:-1], load_edges[1:]):
-            for b in range(CHANNEL_BLOCKS):
+        for k, (first, end) in enumerate(zip(load_edges[:-1], load_edges[1:])):
+            for b in [1, 2, 3, SKIPPED] if k == EARLY_PIECES - 1 else range(CHANNEL_BLOCKS):
                 nc.sync.dma_start(raw[:, b, first:end], wte[b * P : (b + 1) * P, first:end])
 
         offsets = held.tile([P, N // 16], U16, name="offsets")
@@ -56,7 +56,7 @@ def tile_gdw_kernel(tc, wte, offs, out):
 
         for k in range(EARLY_PIECES):
             first, end = load_edges[k : k + 2]
-            for b in range(EARLY_BLOCKS if k == EARLY_PIECES - 1 else CHANNEL_BLOCKS):
+            for b in range(SKIPPED + 1 if k == EARLY_PIECES - 1 else 0, CHANNEL_BLOCKS):
                 sum_words(raw[:, b, first:end], end - first, -1.0 / S, early_sums[:, k, b : b + 1])
 
         def add(x, y, width, name):
@@ -68,13 +68,13 @@ def tile_gdw_kernel(tc, wte, offs, out):
             return raw[:, b, g * BANK : (g + 1) * BANK]
 
         early_total = add(early_sums[:, 0, :], early_sums[:, 1, :], CHANNEL_BLOCKS, "early_total")
-        middle = {b: add(group(b, 1), group(b, 2), BANK, f"middle{b}") for b in range(EARLY_BLOCKS, CHANNEL_BLOCKS)}
+        middle = add(group(SKIPPED, 1), group(SKIPPED, 2), BANK, "middle")
         halves = []
         for b in range(CHANNEL_BLOCKS):
-            late = add(middle[b][:] if b in middle else group(b, 2), group(b, 3), BANK, f"late{b}")
+            late = add(middle[:] if b == SKIPPED else group(b, 2), group(b, 3), BANK, f"late{b}")
             halves.append(add(late[:, : BANK // 2], late[:, BANK // 2 :], BANK // 2, f"half{b}"))
-        third = early_sums[:, EARLY_PIECES - 1, :EARLY_BLOCKS]
-        nc.gpsimd.tensor_add(early_total[:, :EARLY_BLOCKS], early_total[:, :EARLY_BLOCKS], third)
+        third = early_sums[:, EARLY_PIECES - 1, SKIPPED + 1 :]
+        nc.gpsimd.tensor_add(early_total[:, SKIPPED + 1 :], early_total[:, SKIPPED + 1 :], third)
 
         normed = [held.tile([P, C], F32, name=f"normed{j}") for j in range(BLOCKS)]
         flipped, stats, mean_var, rstd, shift = {}, {}, {}, {}, {}
@@ -111,6 +111,18 @@ def tile_gdw_kernel(tc, wte, offs, out):
                 normed[j][:], flipped[j][:], FUNC.Identity, bias=shift[j][:], scale=rstd[p][:, k : k + 1]
             )
 
+        def normalise_last_pair():
+            for k in range(2):
+                j = BLOCKS - 2 + k
+                nc.vector.tensor_scalar(
+                    normed[j][:],
+                    flipped[j][:],
+                    mean_var[PAIRS - 1][:, k, 0:1],
+                    rstd[PAIRS - 1][:, k : k + 1],
+                    ALU.subtract,
+                    ALU.mult,
+                )
+
         e = [held.tile([P, S], F32, name=f"e{b}") for b in range(CHANNEL_BLOCKS)]
 
         def flip_back(b, g, copy):
@@ -134,7 +146,7 @@ def tile_gdw_kernel(tc, wte, offs, out):
                 aggregate_block(j - 1)
                 if j % 2 == 0:
                     root_pair(j // 2 - 1)
-            if j >= 4:
+            if 4 <= j < BLOCKS - 2 + 4:
                 shift_block(j - 4)
                 normalise_block(j - 4)
 
@@ -158,14 +170,16 @@ def tile_gdw_kernel(tc, wte, offs, out):
                 nc.vector.tensor_tensor(picked[:], words, minus_avg_row[b][:, first : first + width], ALU.add)
                 nc.sync.dma_start(out[b * P : (b + 1) * P, first : first + width], picked[:])
 
-        for g in range(GROUPS - 1):
-            flip_back(0, g, nc.vector.tensor_copy)
+        flip_back(0, 0, nc.vector.tensor_copy)
+        flip_back(0, 1, nc.vector.tensor_copy)
+        normalise_last_pair()
+        flip_back(0, 2, nc.vector.tensor_copy)
         flip_back(1, 0, nc.vector.tensor_copy)
         spread_minus_avg(0)
         spread_minus_avg(1)
         flip_back(1, 1, nc.scalar.copy)
         flip_back(1, 2, nc.vector.tensor_copy)
-        flip_back(2, 0, nc.vector.tensor_copy)
+        flip_back(2, 0, nc.scalar.copy)
         flip_back(0, GROUPS - 1, nc.vector.tensor_copy)
         flip_back(1, GROUPS - 1, nc.scalar.copy)
         look_up(0)

@@ -9,6 +9,7 @@ ALU = mybir.AluOpType
 P = 128
 C, S, N = 512, 2048, 512
 EPS = 1e-5
+PIECE = N // 2
 BANK = 512
 PSUM_BANKS = 8
 CHANNEL_BLOCKS = C // P
@@ -25,7 +26,7 @@ def tile_gdw_kernel(tc, wte, offs, out):
     nc = tc.nc
     with (
         tc.tile_pool(name="held", bufs=1) as held,
-        tc.tile_pool(name="rows", bufs=4) as rows,
+        tc.tile_pool(name="rows", bufs=8) as rows,
         tc.tile_pool(name="small", bufs=6) as small,
         tc.psum_pool(name="psum", bufs=PSUM_BANKS) as psum,
     ):
@@ -44,7 +45,7 @@ def tile_gdw_kernel(tc, wte, offs, out):
         nc.vector.memset(eps[:], EPS)
         unused = held.tile([P, 1], F32, name="unused")
         nc.scalar.activation(unused[:], eps[:], FUNC.Abs_reciprocal_sqrt)
-        ones = held.tile([P, N], F32, name="ones")
+        ones = held.tile([P, PIECE], F32, name="ones")
         nc.vector.memset(ones[:], 1.0)
 
         early_sums = held.tile([P, EARLY_PIECES, CHANNEL_BLOCKS], F32, name="early_sums")
@@ -156,19 +157,18 @@ def tile_gdw_kernel(tc, wte, offs, out):
 
         def spread_minus_avg(b):
             sum_words(halves[b][:], BANK // 2, late_scale[:], late_sums[:, b : b + 1])
-            spread = rows.tile([P, N], F32, name="spread")
+            spread = rows.tile([P, PIECE], F32, name="spread")
             nc.gpsimd.tensor_scalar(
                 spread[:], ones[:], late_sums[:, b : b + 1], early_total[:, b : b + 1], ALU.mult, ALU.add
             )
             minus_avg_row.append(spread)
 
-        def look_up(b, pieces=1):
-            width = N // pieces
-            for first in range(0, N, width):
-                picked = rows.tile([P, width], F32, name="picked")
-                words = e[b][:].indirect(offsets[:, first // 16 : (first + width) // 16])
-                nc.vector.tensor_tensor(picked[:], words, minus_avg_row[b][:, first : first + width], ALU.add)
-                nc.sync.dma_start(out[b * P : (b + 1) * P, first : first + width], picked[:])
+        def look_up(b):
+            for first in range(0, N, PIECE):
+                picked = rows.tile([P, PIECE], F32, name="picked")
+                words = e[b][:].indirect(offsets[:, first // 16 : (first + PIECE) // 16])
+                nc.vector.tensor_tensor(picked[:], words, minus_avg_row[b][:], ALU.add)
+                nc.sync.dma_start(out[b * P : (b + 1) * P, first : first + PIECE], picked[:])
 
         flip_back(0, 0, nc.vector.tensor_copy)
         flip_back(0, 1, nc.vector.tensor_copy)
@@ -192,4 +192,4 @@ def tile_gdw_kernel(tc, wte, offs, out):
         for g in range(1, GROUPS):
             flip_back(3, g, nc.scalar.copy)
         look_up(2)
-        look_up(3, pieces=2)
+        look_up(3)

@@ -18,8 +18,8 @@ BLOCKS_IN_GROUP = BANK // P
 BLOCKS = S // P
 PAIRS = BLOCKS // 2
 FLIP_AHEAD = 3
-EARLY_PIECES = 3
-SKIPPED = 0
+EARLY_EDGES = [0, BANK // 2, BANK, 2 * BANK]
+SKIPPED = 2
 
 
 def tile_gdw_kernel(tc, wte, offs, out):
@@ -31,9 +31,9 @@ def tile_gdw_kernel(tc, wte, offs, out):
         tc.psum_pool(name="psum", bufs=PSUM_BANKS) as psum,
     ):
         raw = held.tile([P, CHANNEL_BLOCKS, S], F32, name="raw")
-        load_edges = [0, BANK // 2] + [g * BANK for g in range(1, GROUPS + 1)]
+        load_edges = [0, 2 * P, 5 * P] + [g * BANK for g in range(2, GROUPS + 1)]
         for k, (first, end) in enumerate(zip(load_edges[:-1], load_edges[1:])):
-            for b in [1, 2, 3, SKIPPED] if k == EARLY_PIECES - 1 else range(CHANNEL_BLOCKS):
+            for b in [2, 3, 0, 1] if k == 2 else range(CHANNEL_BLOCKS):
                 nc.sync.dma_start(raw[:, b, first:end], wte[b * P : (b + 1) * P, first:end])
 
         offsets = held.tile([P, N // 16], U16, name="offsets")
@@ -43,22 +43,22 @@ def tile_gdw_kernel(tc, wte, offs, out):
         make_identity(nc, identity[:])
         eps = held.tile([P, 1], F32, name="eps")
         nc.vector.memset(eps[:], EPS)
-        unused = held.tile([P, 1], F32, name="unused")
-        nc.scalar.activation(unused[:], eps[:], FUNC.Abs_reciprocal_sqrt)
+        warm = held.tile([P, 1], F32, name="warm")
+        nc.scalar.activation(warm[:], eps[:], FUNC.Abs_reciprocal_sqrt)
         ones = held.tile([P, PIECE], F32, name="ones")
         nc.vector.memset(ones[:], 1.0)
 
-        early_sums = held.tile([P, EARLY_PIECES, CHANNEL_BLOCKS], F32, name="early_sums")
+        early_sums = held.tile([P, 3, CHANNEL_BLOCKS], F32, name="early_sums")
         late_sums = held.tile([P, CHANNEL_BLOCKS], F32, name="late_sums")
 
-        def sum_words(words, width, scale, total):
-            scaled = rows.tile([P, BANK], F32, name="scaled")
-            nc.scalar.activation(scaled[:, :width], words, FUNC.Copy, scale=scale, accum_out=total)
+        def sum_words(words, unused, scale, total):
+            nc.scalar.activation(unused, words, FUNC.Copy, scale=scale, accum_out=total)
 
-        for k in range(EARLY_PIECES):
-            first, end = load_edges[k : k + 2]
-            for b in range(SKIPPED + 1 if k == EARLY_PIECES - 1 else 0, CHANNEL_BLOCKS):
-                sum_words(raw[:, b, first:end], end - first, -1.0 / S, early_sums[:, k, b : b + 1])
+        for k in range(3):
+            first, end = EARLY_EDGES[k : k + 2]
+            for b in range(SKIPPED if k == 2 else 0, CHANNEL_BLOCKS):
+                unused = rows.tile([P, BANK], F32, name="unused")
+                sum_words(raw[:, b, first:end], unused[:, : end - first], -1.0 / S, early_sums[:, k, b : b + 1])
 
         def add(x, y, width, name):
             added = held.tile([P, width], F32, name=name)
@@ -69,13 +69,13 @@ def tile_gdw_kernel(tc, wte, offs, out):
             return raw[:, b, g * BANK : (g + 1) * BANK]
 
         early_total = add(early_sums[:, 0, :], early_sums[:, 1, :], CHANNEL_BLOCKS, "early_total")
-        middle = add(group(SKIPPED, 1), group(SKIPPED, 2), BANK, "middle")
+        middle = [add(group(b, 1), group(b, 2), BANK, f"middle{b}") for b in range(SKIPPED)]
         halves = []
         for b in range(CHANNEL_BLOCKS):
-            late = add(middle[:] if b == SKIPPED else group(b, 2), group(b, 3), BANK, f"late{b}")
+            late = add(middle[b][:] if b < SKIPPED else group(b, 2), group(b, 3), BANK, f"late{b}")
             halves.append(add(late[:, : BANK // 2], late[:, BANK // 2 :], BANK // 2, f"half{b}"))
-        third = early_sums[:, EARLY_PIECES - 1, SKIPPED + 1 :]
-        nc.gpsimd.tensor_add(early_total[:, SKIPPED + 1 :], early_total[:, SKIPPED + 1 :], third)
+        third = early_sums[:, 2, SKIPPED:]
+        nc.gpsimd.tensor_add(early_total[:, SKIPPED:], early_total[:, SKIPPED:], third)
 
         normed = [held.tile([P, C], F32, name=f"normed{j}") for j in range(BLOCKS)]
         flipped, stats, mean_var, rstd, shift = {}, {}, {}, {}, {}
@@ -156,7 +156,11 @@ def tile_gdw_kernel(tc, wte, offs, out):
         minus_avg_row = []
 
         def spread_minus_avg(b):
-            sum_words(halves[b][:], BANK // 2, late_scale[:], late_sums[:, b : b + 1])
+            if b < 2:
+                unused = rows.tile([P, BANK], F32, name="unused")
+            else:
+                unused = normed[BLOCKS - 4 + b]
+            sum_words(halves[b][:], unused[:, : BANK // 2], late_scale[:], late_sums[:, b : b + 1])
             spread = rows.tile([P, PIECE], F32, name="spread")
             nc.gpsimd.tensor_scalar(
                 spread[:], ones[:], late_sums[:, b : b + 1], early_total[:, b : b + 1], ALU.mult, ALU.add

import concourse.mybir as mybir
from concourse.masks import make_identity

F32 = mybir.dt.float32
U16 = mybir.dt.uint16
FUNC = mybir.ActivationFunctionType
ALU = mybir.AluOpType

P = 128
C, S, N = 512, 2048, 512
EPS = 1e-5
PIECE = N // 2
BANK = 512
PSUM_BANKS = 8
CHANNEL_BLOCKS = C // P
GROUPS = S // BANK
BLOCKS_IN_GROUP = BANK // P
BLOCKS = S // P
PAIRS = BLOCKS // 2
FLIP_AHEAD = 3
EARLY_EDGES = [0, BANK // 2, BANK, 2 * BANK]
SKIPPED = 2


def tile_gdw_kernel(tc, wte, offs, out):
    nc = tc.nc
    with (
        tc.tile_pool(name="held", bufs=1) as held,
        tc.tile_pool(name="rows", bufs=8) as rows,
        tc.tile_pool(name="small", bufs=6) as small,
        tc.psum_pool(name="psum", bufs=PSUM_BANKS) as psum,
    ):
        raw = held.tile([P, CHANNEL_BLOCKS, S], F32, name="raw")
        load_edges = [0, 2 * P, 5 * P] + [g * BANK for g in range(2, GROUPS + 1)]
        for k, (first, end) in enumerate(zip(load_edges[:-1], load_edges[1:])):
            for b in [2, 3, 0, 1] if k == 2 else range(CHANNEL_BLOCKS):
                nc.sync.dma_start(raw[:, b, first:end], wte[b * P : (b + 1) * P, first:end])

        offsets = held.tile([P, N // 16], U16, name="offsets")
        nc.sync.dma_start(offsets[:], offs)

        identity = held.tile([P, P], F32, name="identity")
        make_identity(nc, identity[:])
        eps = held.tile([P, 1], F32, name="eps")
        nc.vector.memset(eps[:], EPS)
        warm = held.tile([P, 1], F32, name="warm")
        nc.scalar.activation(warm[:], eps[:], FUNC.Abs_reciprocal_sqrt)
        ones = held.tile([P, PIECE], F32, name="ones")
        nc.vector.memset(ones[:], 1.0)

        early_sums = held.tile([P, 3, CHANNEL_BLOCKS], F32, name="early_sums")
        late_sums = held.tile([P, CHANNEL_BLOCKS], F32, name="late_sums")

        def sum_words(words, unused, scale, total):
            nc.scalar.activation(unused, words, FUNC.Copy, scale=scale, accum_out=total)

        for k in range(3):
            first, end = EARLY_EDGES[k : k + 2]
            for b in range(SKIPPED if k == 2 else 0, CHANNEL_BLOCKS):
                unused = rows.tile([P, BANK], F32, name="unused")
                sum_words(raw[:, b, first:end], unused[:, : end - first], -1.0 / S, early_sums[:, k, b : b + 1])

        def add(x, y, width, name):
            added = held.tile([P, width], F32, name=name)
            nc.gpsimd.tensor_add(added[:], x, y)
            return added

        def group(b, g):
            return raw[:, b, g * BANK : (g + 1) * BANK]

        early_total = add(early_sums[:, 0, :], early_sums[:, 1, :], CHANNEL_BLOCKS, "early_total")
        middle = [add(group(b, 1), group(b, 2), BANK, f"middle{b}") for b in range(SKIPPED)]
        halves = []
        for b in range(CHANNEL_BLOCKS):
            late = add(middle[b][:] if b < SKIPPED else group(b, 2), group(b, 3), BANK, f"late{b}")
            halves.append(add(late[:, : BANK // 2], late[:, BANK // 2 :], BANK // 2, f"half{b}"))
        third = early_sums[:, 2, SKIPPED:]
        nc.gpsimd.tensor_add(early_total[:, SKIPPED:], early_total[:, SKIPPED:], third)

        normed = [held.tile([P, C], F32, name=f"normed{j}") for j in range(BLOCKS)]
        flipped, stats, mean_var, rstd, shift = {}, {}, {}, {}, {}

        def flip_block(j):
            flipped[j] = psum.tile([P, C], F32, name="bank")
            for b in range(CHANNEL_BLOCKS):
                nc.tensor.transpose(flipped[j][:, b * P : (b + 1) * P], raw[:, b, j * P : (j + 1) * P], identity[:])

        def measure_block(j):
            stats[j] = small.tile([P, 6], F32, name="stats")
            nc.vector.bn_stats(stats[j][:], flipped[j][:])

        def aggregate_block(j):
            p, k = divmod(j, 2)
            if k == 0:
                mean_var[p] = small.tile([P, 2, 2], F32, name="mean_var")
            nc.vector.bn_aggr(mean_var[p][:, k, :], stats[j][:])

        def root_pair(p):
            rstd[p] = small.tile([P, 2], F32, name="rstd")
            nc.scalar.activation(rstd[p][:], mean_var[p][:, :, 1], FUNC.Abs_reciprocal_sqrt, bias=eps[:])

        def shift_block(j):
            p, k = divmod(j, 2)
            shift[j] = small.tile([P, 1], F32, name="shift")
            nc.vector.tensor_scalar(
                shift[j][:], mean_var[p][:, k, 0:1], rstd[p][:, k : k + 1], -1.0, ALU.mult, ALU.mult
            )

        def normalise_block(j):
            p, k = divmod(j, 2)
            nc.scalar.activation(
                normed[j][:], flipped[j][:], FUNC.Identity, bias=shift[j][:], scale=rstd[p][:, k : k + 1]
            )

        def normalise_last_pair():
            for k in range(2):
                j = BLOCKS - 2 + k
                nc.vector.tensor_scalar(
                    normed[j][:],
                    flipped[j][:],
                    mean_var[PAIRS - 1][:, k, 0:1],
                    rstd[PAIRS - 1][:, k : k + 1],
                    ALU.subtract,
                    ALU.mult,
                )

        e = [held.tile([P, S], F32, name=f"e{b}") for b in range(CHANNEL_BLOCKS)]

        def flip_back(b, g, copy):
            e_bank = psum.tile([P, BANK], F32, name="bank")
            for i in range(BLOCKS_IN_GROUP):
                nc.tensor.transpose(
                    e_bank[:, i * P : (i + 1) * P],
                    normed[g * BLOCKS_IN_GROUP + i][:, b * P : (b + 1) * P],
                    identity[:],
                )
            copy(e[b][:, g * BANK : (g + 1) * BANK], e_bank[:])

        for j in range(FLIP_AHEAD):
            flip_block(j)
        for j in range(BLOCKS + 4):
            if j + FLIP_AHEAD < BLOCKS:
                flip_block(j + FLIP_AHEAD)
            if j < BLOCKS:
                measure_block(j)
            if 1 <= j <= BLOCKS:
                aggregate_block(j - 1)
                if j % 2 == 0:
                    root_pair(j // 2 - 1)
            if 4 <= j < BLOCKS - 2 + 4:
                shift_block(j - 4)
                normalise_block(j - 4)

        late_scale = held.tile([P, 1], F32, name="late_scale")
        nc.vector.tensor_scalar(late_scale[:], stats[BLOCKS - 1][:, 0:1], -1.0 / (S * (C // 2)), 0.0, ALU.mult, ALU.add)
        minus_avg_row = []

        def spread_minus_avg(b):
            if b < 2:
                unused = rows.tile([P, BANK], F32, name="unused")
            else:
                unused = normed[BLOCKS - 4 + b]
            sum_words(halves[b][:], unused[:, : BANK // 2], late_scale[:], late_sums[:, b : b + 1])
            spread = rows.tile([P, PIECE], F32, name="spread")
            nc.gpsimd.tensor_scalar(
                spread[:], ones[:], late_sums[:, b : b + 1], early_total[:, b : b + 1], ALU.mult, ALU.add
            )
            minus_avg_row.append(spread)

        def look_up(b):
            for first in range(0, N, PIECE):
                picked = rows.tile([P, PIECE], F32, name="picked")
                words = e[b][:].indirect(offsets[:, first // 16 : (first + PIECE) // 16])
                nc.vector.tensor_tensor(picked[:], words, minus_avg_row[b][:], ALU.add)
                nc.sync.dma_start(out[b * P : (b + 1) * P, first : first + PIECE], picked[:])

        flip_back(0, 0, nc.vector.tensor_copy)
        flip_back(0, 1, nc.vector.tensor_copy)
        normalise_last_pair()
        flip_back(0, 2, nc.vector.tensor_copy)
        flip_back(1, 0, nc.vector.tensor_copy)
        spread_minus_avg(0)
        spread_minus_avg(1)
        flip_back(1, 1, nc.scalar.copy)
        flip_back(1, 2, nc.vector.tensor_copy)
        flip_back(2, 0, nc.scalar.copy)
        flip_back(0, GROUPS - 1, nc.vector.tensor_copy)
        flip_back(1, GROUPS - 1, nc.scalar.copy)
        look_up(0)
        spread_minus_avg(2)
        spread_minus_avg(3)
        for g in range(1, GROUPS):
            flip_back(2, g, nc.scalar.copy)
        look_up(1)
        flip_back(3, 0, nc.vector.tensor_copy)
        for g in range(1, GROUPS):
            flip_back(3, g, nc.scalar.copy)
        look_up(2)
        look_up(3)
